import numpy as np
import ml_dtypes

BF16 = ml_dtypes.bfloat16


def bf(x):
    return np.asarray(x, np.float32).astype(BF16)


def f32(x):
    return np.asarray(x, np.float32)


def f64(x):
    return np.asarray(x).astype(np.float64)


def striped(idx):
    return np.tile(idx.reshape(-1, 16).T, (8, 1))


E, S, N, HD, HALF, MR, M = 128, 256, 128, 128, 64, 384, 512
ATT = 0.1 * np.log(2.0) + 1.0


def setup_inputs():
    x = bf(np.random.standard_normal((E, S)))
    w = bf(np.random.standard_normal((E, M)) / np.sqrt(E))
    b = f32(0.1 * np.random.standard_normal((M, 1)))
    ang = np.random.uniform(0.0, 2.0 * np.pi, (HALF, N))
    ang = np.concatenate([ang, ang], axis=0)
    return {"x": x, "w": w, "b": b, "cosn": f32(ATT * np.cos(ang)), "sinn": f32(ATT * np.sin(ang)), "offs": striped(np.random.permutation(S)[:N])}


def reference(x, w, b, cosn, sinn, offs):
    idx = offs[:16].T.reshape(-1)
    y = f64(w).T @ f64(x)[:, idx] + f64(b)
    t = y[:MR].reshape(-1, HD, N)
    rot = np.concatenate([-t[:, HALF:], t[:, :HALF]], axis=1)
    r = t * f64(cosn)[None] + rot * f64(sinn)[None]
    return np.concatenate([r.reshape(MR, N), y[MR:]], axis=0)

@@ -1,0 +1,73 @@
+import concourse.mybir as mybir
+
+BF16, F32, U16 = mybir.dt.bfloat16, mybir.dt.float32, mybir.dt.uint16
+ADD, MULT = mybir.AluOpType.add, mybir.AluOpType.mult
+IDENTITY = mybir.ActivationFunctionType.Identity
+
+E = 128
+S = 256
+N = 128
+HD = 128
+HALF = HD // 2
+ROPE_HEADS = 3
+HEADS = ROPE_HEADS + 1
+
+FLOPS = 2 * E * HEADS * HD * N
+
+
+def tile_groupqueryattention_kernel(tc, x, w, b, cosn, sinn, offs, out):
+    nc = tc.nc
+    with (
+        tc.tile_pool(name="held", bufs=1) as held,
+        tc.tile_pool(name="work", bufs=ROPE_HEADS) as work,
+        tc.psum_pool(name="psum", bufs=1) as psum,
+    ):
+        offsets = held.tile([E, N // 16], U16, name="offsets")
+        nc.sync.dma_start(offsets[:], offs)
+        tokens = held.tile([E, S], BF16, name="tokens")
+        nc.sync.dma_start(tokens[:], x)
+
+        w_rope = held.tile([E, ROPE_HEADS, HD + HALF], BF16, name="w_rope")
+        w_by_head = w.rearrange("k (h d) -> k h d", d=HD)
+        nc.scalar.dma_start(w_rope[:, :, 0:HD], w_by_head[:, 0:ROPE_HEADS, :])
+        nc.scalar.dma_start(w_rope[:, :, HD : HD + HALF], w_by_head[:, 0:ROPE_HEADS, 0:HALF])
+        w_value = held.tile([E, HD], BF16, name="w_value")
+        nc.scalar.dma_start(w_value[:], w_by_head[:, ROPE_HEADS, :])
+
+        sin_signed = held.tile([HD, N], F32, name="sin_signed")
+        nc.gpsimd.dma_start(sin_signed[:], sinn)
+        cos = held.tile([HD, N], F32, name="cos")
+        nc.gpsimd.dma_start(cos[:], cosn)
+
+        bias = held.tile([HD, HEADS], F32, name="bias")
+        bias_swapped = held.tile([HD, ROPE_HEADS], F32, name="bias_swapped")
+        b_halves = b.rearrange("(h t p) o -> t p (h o)", t=2, p=HALF)
+        with nc.allow_non_contiguous_dma(reason="one float32 of the bias to a partition"):
+            nc.sync.dma_start(bias[:], b.rearrange("(h p) o -> p (h o)", p=HD))
+            nc.sync.dma_start(bias_swapped[0:HALF, :], b_halves[1][:, 0:ROPE_HEADS])
+            nc.sync.dma_start(bias_swapped[HALF:HD, :], b_halves[0][:, 0:ROPE_HEADS])
+
+        nc.vector.tensor_scalar_mul(sin_signed[0:HALF, :], sin_signed[0:HALF, :], -1.0)
+
+        picked = tokens[:].indirect(offsets[:])
+        value_ps = psum.tile([HD, N], F32, name="value_ps")
+        nc.tensor.matmul(value_ps[:], w_value[:], picked, start=True, stop=True)
+        value = held.tile([HD, N], F32, name="value")
+        nc.scalar.activation(value[:], value_ps[:], IDENTITY, bias=bias[:, ROPE_HEADS : ROPE_HEADS + 1])
+        nc.scalar.dma_start(out[ROPE_HEADS * HD : HEADS * HD, :], value[:])
+
+        for h in range(ROPE_HEADS):
+            straight_ps = psum.tile([HD, N], F32, name=f"straight_ps{h}")
+            nc.tensor.matmul(straight_ps[:], w_rope[:, h, 0:HD], picked, start=True, stop=True)
+            swapped_ps = psum.tile([HD, N], F32, name=f"swapped_ps{h}")
+            nc.tensor.matmul(swapped_ps[:], w_rope[:, h, HALF : HALF + HD], picked, start=True, stop=True)
+
+            by_cos = work.tile([HD, N], F32, name="by_cos")
+            nc.vector.scalar_tensor_tensor(by_cos[:], straight_ps[:], bias[:, h : h + 1], cos[:], ADD, MULT)
+            by_sin = work.tile([HD, N], F32, name="by_sin")
+            nc.vector.scalar_tensor_tensor(
+                by_sin[:], swapped_ps[:], bias_swapped[:, h : h + 1], sin_signed[:], ADD, MULT
+            )
+            rotated = work.tile([HD, N], F32, name="rotated")
+            nc.vector.tensor_tensor(rotated[:], by_cos[:], by_sin[:], ADD)
+            nc.sync.dma_start(out[h * HD : (h + 1) * HD, :], rotated[:])

@@ -35,9 +35,9 @@ def tile_groupqueryattention_kernel(tc, x, w, b, cosn, sinn, offs, out):
         nc.scalar.dma_start(w_value[:], w_by_head[:, ROPE_HEADS, :])
 
         sin_signed = held.tile([HD, N], F32, name="sin_signed")
-        nc.gpsimd.dma_start(sin_signed[:], sinn)
+        nc.scalar.dma_start(sin_signed[:], sinn)
         cos = held.tile([HD, N], F32, name="cos")
-        nc.gpsimd.dma_start(cos[:], cosn)
+        nc.sync.dma_start(cos[:], cosn)
 
         bias = held.tile([HD, HEADS], F32, name="bias")
         bias_swapped = held.tile([HD, ROPE_HEADS], F32, name="bias_swapped")

@@ -47,6 +47,10 @@ def tile_groupqueryattention_kernel(tc, x, w, b, cosn, sinn, offs, out):
             nc.sync.dma_start(bias_swapped[0:HALF, :], b_halves[1][:, 0:ROPE_HEADS])
             nc.sync.dma_start(bias_swapped[HALF:HD, :], b_halves[0][:, 0:ROPE_HEADS])
 
+        scratch = held.tile([HD, 1], F32, name="scratch")
+        nc.vector.memset(scratch[:], 0.0)
+        nc.scalar.activation(scratch[:], scratch[:], IDENTITY)
+
         nc.vector.tensor_scalar_mul(sin_signed[0:HALF, :], sin_signed[0:HALF, :], -1.0)
 
         picked = tokens[:].indirect(offsets[:])

@@ -1,4 +1,5 @@
 import concourse.mybir as mybir
+from concourse.masks import make_identity
 
 BF16, F32, U16 = mybir.dt.bfloat16, mybir.dt.float32, mybir.dt.uint16
 ADD, MULT = mybir.AluOpType.add, mybir.AluOpType.mult
@@ -24,6 +25,10 @@ def tile_groupqueryattention_kernel(tc, x, w, b, cosn, sinn, offs, out):
     ):
         offsets = held.tile([E, N // 16], U16, name="offsets")
         nc.sync.dma_start(offsets[:], offs)
+        b_rows = held.tile([HEADS, HD + HALF], F32, name="b_rows")
+        b_by_head = b.rearrange("(h p) o -> h (p o)", p=HD)
+        nc.sync.dma_start(b_rows[:, 0:HD], b_by_head)
+        nc.sync.dma_start(b_rows[:, HD : HD + HALF], b_by_head[:, 0:HALF])
         tokens = held.tile([E, S], BF16, name="tokens")
         nc.sync.dma_start(tokens[:], x)
 
@@ -39,13 +44,13 @@ def tile_groupqueryattention_kernel(tc, x, w, b, cosn, sinn, offs, out):
         cos = held.tile([HD, N], F32, name="cos")
         nc.sync.dma_start(cos[:], cosn)
 
-        bias = held.tile([HD, HEADS], F32, name="bias")
-        bias_swapped = held.tile([HD, ROPE_HEADS], F32, name="bias_swapped")
-        b_halves = b.rearrange("(h t p) o -> t p (h o)", t=2, p=HALF)
-        with nc.allow_non_contiguous_dma(reason="one float32 of the bias to a partition"):
-            nc.sync.dma_start(bias[:], b.rearrange("(h p) o -> p (h o)", p=HD))
-            nc.sync.dma_start(bias_swapped[0:HALF, :], b_halves[1][:, 0:ROPE_HEADS])
-            nc.sync.dma_start(bias_swapped[HALF:HD, :], b_halves[0][:, 0:ROPE_HEADS])
+        identity = held.tile([HEADS, HEADS], F32, name="identity")
+        make_identity(nc, identity[:])
+        bias_ps = psum.tile([HD, 2 * HEADS], F32, name="bias_ps")
+        nc.tensor.matmul(bias_ps[:, 0:HEADS], b_rows[:, 0:HD], identity[:], start=True, stop=True)
+        nc.tensor.matmul(bias_ps[:, HEADS : 2 * HEADS], b_rows[:, HALF : HALF + HD], identity[:], start=True, stop=True)
+        bias = held.tile([HD, 2 * HEADS], F32, name="bias")
+        nc.vector.tensor_copy(bias[:], bias_ps[:])
 
         scratch = held.tile([HD, 1], F32, name="scratch")
         nc.vector.memset(scratch[:], 0.0)
@@ -70,7 +75,7 @@ def tile_groupqueryattention_kernel(tc, x, w, b, cosn, sinn, offs, out):
             nc.vector.scalar_tensor_tensor(by_cos[:], straight_ps[:], bias[:, h : h + 1], cos[:], ADD, MULT)
             by_sin = work.tile([HD, N], F32, name="by_sin")
             nc.vector.scalar_tensor_tensor(
-                by_sin[:], swapped_ps[:], bias_swapped[:, h : h + 1], sin_signed[:], ADD, MULT
+                by_sin[:], swapped_ps[:], bias[:, HEADS + h : HEADS + h + 1], sin_signed[:], ADD, MULT
             )
             rotated = work.tile([HD, N], F32, name="rotated")
             nc.vector.tensor_tensor(rotated[:], by_cos[:], by_sin[:], ADD)

@@ -1,5 +1,4 @@
 import concourse.mybir as mybir
-from concourse.masks import make_identity
 
 BF16, F32, U16 = mybir.dt.bfloat16, mybir.dt.float32, mybir.dt.uint16
 ADD, MULT = mybir.AluOpType.add, mybir.AluOpType.mult
@@ -13,6 +12,9 @@ HALF = HD // 2
 ROPE_HEADS = 3
 HEADS = ROPE_HEADS + 1
 
+BANK = 512
+WARM_UPS = 6
+
 FLOPS = 2 * E * HEADS * HD * N
 
 
@@ -23,12 +25,14 @@ def tile_groupqueryattention_kernel(tc, x, w, b, cosn, sinn, offs, out):
         tc.tile_pool(name="work", bufs=ROPE_HEADS) as work,
         tc.psum_pool(name="psum", bufs=1) as psum,
     ):
+        zeros = held.tile([E, BANK], BF16, name="zeros")
+        nc.vector.memset(zeros[:], 0.0)
+        warm_ps = psum.tile([HD, BANK], F32, name="warm_ps")
+        for i in range(WARM_UPS):
+            nc.tensor.matmul(warm_ps[:], zeros[:, 0:HD], zeros[:], start=True, stop=True)
+
         offsets = held.tile([E, N // 16], U16, name="offsets")
         nc.sync.dma_start(offsets[:], offs)
-        b_rows = held.tile([HEADS, HD + HALF], F32, name="b_rows")
-        b_by_head = b.rearrange("(h p) o -> h (p o)", p=HD)
-        nc.sync.dma_start(b_rows[:, 0:HD], b_by_head)
-        nc.sync.dma_start(b_rows[:, HD : HD + HALF], b_by_head[:, 0:HALF])
         tokens = held.tile([E, S], BF16, name="tokens")
         nc.sync.dma_start(tokens[:], x)
 
@@ -44,13 +48,13 @@ def tile_groupqueryattention_kernel(tc, x, w, b, cosn, sinn, offs, out):
         cos = held.tile([HD, N], F32, name="cos")
         nc.sync.dma_start(cos[:], cosn)
 
-        identity = held.tile([HEADS, HEADS], F32, name="identity")
-        make_identity(nc, identity[:])
-        bias_ps = psum.tile([HD, 2 * HEADS], F32, name="bias_ps")
-        nc.tensor.matmul(bias_ps[:, 0:HEADS], b_rows[:, 0:HD], identity[:], start=True, stop=True)
-        nc.tensor.matmul(bias_ps[:, HEADS : 2 * HEADS], b_rows[:, HALF : HALF + HD], identity[:], start=True, stop=True)
-        bias = held.tile([HD, 2 * HEADS], F32, name="bias")
-        nc.vector.tensor_copy(bias[:], bias_ps[:])
+        bias = held.tile([HD, HEADS], F32, name="bias")
+        bias_swapped = held.tile([HD, ROPE_HEADS], F32, name="bias_swapped")
+        b_halves = b.rearrange("(h t p) o -> t p (h o)", t=2, p=HALF)
+        with nc.allow_non_contiguous_dma(reason="one float32 of the bias to a partition"):
+            nc.sync.dma_start(bias[:], b.rearrange("(h p) o -> p (h o)", p=HD))
+            nc.sync.dma_start(bias_swapped[0:HALF, :], b_halves[1][:, 0:ROPE_HEADS])
+            nc.sync.dma_start(bias_swapped[HALF:HD, :], b_halves[0][:, 0:ROPE_HEADS])
 
         scratch = held.tile([HD, 1], F32, name="scratch")
         nc.vector.memset(scratch[:], 0.0)
@@ -75,7 +79,7 @@ def tile_groupqueryattention_kernel(tc, x, w, b, cosn, sinn, offs, out):
             nc.vector.scalar_tensor_tensor(by_cos[:], straight_ps[:], bias[:, h : h + 1], cos[:], ADD, MULT)
             by_sin = work.tile([HD, N], F32, name="by_sin")
             nc.vector.scalar_tensor_tensor(
-                by_sin[:], swapped_ps[:], bias[:, HEADS + h : HEADS + h + 1], sin_signed[:], ADD, MULT
+                by_sin[:], swapped_ps[:], bias_swapped[:, h : h + 1], sin_signed[:], ADD, MULT
             )
             rotated = work.tile([HD, N], F32, name="rotated")
             nc.vector.tensor_tensor(rotated[:], by_cos[:], by_sin[:], ADD)

@@ -12,9 +12,6 @@ HALF = HD // 2
 ROPE_HEADS = 3
 HEADS = ROPE_HEADS + 1
 
-BANK = 512
-WARM_UPS = 6
-
 FLOPS = 2 * E * HEADS * HD * N
 
 
@@ -25,23 +22,16 @@ def tile_groupqueryattention_kernel(tc, x, w, b, cosn, sinn, offs, out):
         tc.tile_pool(name="work", bufs=ROPE_HEADS) as work,
         tc.psum_pool(name="psum", bufs=1) as psum,
     ):
-        zeros = held.tile([E, BANK], BF16, name="zeros")
-        nc.vector.memset(zeros[:], 0.0)
-        warm_ps = psum.tile([HD, BANK], F32, name="warm_ps")
-        for i in range(WARM_UPS):
-            nc.tensor.matmul(warm_ps[:], zeros[:, 0:HD], zeros[:], start=True, stop=True)
-
         offsets = held.tile([E, N // 16], U16, name="offsets")
         nc.sync.dma_start(offsets[:], offs)
         tokens = held.tile([E, S], BF16, name="tokens")
         nc.sync.dma_start(tokens[:], x)
 
-        w_rope = held.tile([E, ROPE_HEADS, HD + HALF], BF16, name="w_rope")
-        w_by_head = w.rearrange("k (h d) -> k h d", d=HD)
-        nc.scalar.dma_start(w_rope[:, :, 0:HD], w_by_head[:, 0:ROPE_HEADS, :])
-        nc.scalar.dma_start(w_rope[:, :, HD : HD + HALF], w_by_head[:, 0:ROPE_HEADS, 0:HALF])
-        w_value = held.tile([E, HD], BF16, name="w_value")
-        nc.scalar.dma_start(w_value[:], w_by_head[:, ROPE_HEADS, :])
+        weights = held.tile([E, HEADS, HD], BF16, name="weights")
+        nc.scalar.dma_start(weights[:], w.rearrange("k (h d) -> k h d", d=HD))
+        w_swapped = held.tile([E, ROPE_HEADS, HD], BF16, name="w_swapped")
+        nc.vector.tensor_copy(w_swapped[:, :, 0:HALF], weights[:, 0:ROPE_HEADS, HALF:HD])
+        nc.vector.tensor_copy(w_swapped[:, :, HALF:HD], weights[:, 0:ROPE_HEADS, 0:HALF])
 
         sin_signed = held.tile([HD, N], F32, name="sin_signed")
         nc.scalar.dma_start(sin_signed[:], sinn)
@@ -53,8 +43,8 @@ def tile_groupqueryattention_kernel(tc, x, w, b, cosn, sinn, offs, out):
         b_halves = b.rearrange("(h t p) o -> t p (h o)", t=2, p=HALF)
         with nc.allow_non_contiguous_dma(reason="one float32 of the bias to a partition"):
             nc.sync.dma_start(bias[:], b.rearrange("(h p) o -> p (h o)", p=HD))
-            nc.sync.dma_start(bias_swapped[0:HALF, :], b_halves[1][:, 0:ROPE_HEADS])
-            nc.sync.dma_start(bias_swapped[HALF:HD, :], b_halves[0][:, 0:ROPE_HEADS])
+            nc.scalar.dma_start(bias_swapped[0:HALF, :], b_halves[1][:, 0:ROPE_HEADS])
+            nc.scalar.dma_start(bias_swapped[HALF:HD, :], b_halves[0][:, 0:ROPE_HEADS])
 
         scratch = held.tile([HD, 1], F32, name="scratch")
         nc.vector.memset(scratch[:], 0.0)
@@ -63,24 +53,26 @@ def tile_groupqueryattention_kernel(tc, x, w, b, cosn, sinn, offs, out):
         nc.vector.tensor_scalar_mul(sin_signed[0:HALF, :], sin_signed[0:HALF, :], -1.0)
 
         picked = tokens[:].indirect(offsets[:])
-        value_ps = psum.tile([HD, N], F32, name="value_ps")
-        nc.tensor.matmul(value_ps[:], w_value[:], picked, start=True, stop=True)
-        value = held.tile([HD, N], F32, name="value")
-        nc.scalar.activation(value[:], value_ps[:], IDENTITY, bias=bias[:, ROPE_HEADS : ROPE_HEADS + 1])
-        nc.scalar.dma_start(out[ROPE_HEADS * HD : HEADS * HD, :], value[:])
-
+        by_cos = []
         for h in range(ROPE_HEADS):
             straight_ps = psum.tile([HD, N], F32, name=f"straight_ps{h}")
-            nc.tensor.matmul(straight_ps[:], w_rope[:, h, 0:HD], picked, start=True, stop=True)
-            swapped_ps = psum.tile([HD, N], F32, name=f"swapped_ps{h}")
-            nc.tensor.matmul(swapped_ps[:], w_rope[:, h, HALF : HALF + HD], picked, start=True, stop=True)
+            nc.tensor.matmul(straight_ps[:], weights[:, h, :], picked, start=True, stop=True)
+            by_cos.append(work.tile([HD, N], F32, name="by_cos"))
+            nc.vector.scalar_tensor_tensor(by_cos[h][:], straight_ps[:], bias[:, h : h + 1], cos[:], ADD, MULT)
 
-            by_cos = work.tile([HD, N], F32, name="by_cos")
-            nc.vector.scalar_tensor_tensor(by_cos[:], straight_ps[:], bias[:, h : h + 1], cos[:], ADD, MULT)
+        for h in range(ROPE_HEADS):
+            swapped_ps = psum.tile([HD, N], F32, name=f"swapped_ps{h}")
+            nc.tensor.matmul(swapped_ps[:], w_swapped[:, h, :], picked, start=True, stop=True)
             by_sin = work.tile([HD, N], F32, name="by_sin")
             nc.vector.scalar_tensor_tensor(
                 by_sin[:], swapped_ps[:], bias_swapped[:, h : h + 1], sin_signed[:], ADD, MULT
             )
             rotated = work.tile([HD, N], F32, name="rotated")
-            nc.vector.tensor_tensor(rotated[:], by_cos[:], by_sin[:], ADD)
+            nc.vector.tensor_tensor(rotated[:], by_cos[h][:], by_sin[:], ADD)
             nc.sync.dma_start(out[h * HD : (h + 1) * HD, :], rotated[:])
+
+        value_ps = psum.tile([HD, N], F32, name="value_ps")
+        nc.tensor.matmul(value_ps[:], weights[:, ROPE_HEADS, :], picked, start=True, stop=True)
+        value = held.tile([HD, N], F32, name="value")
+        nc.scalar.activation(value[:], value_ps[:], IDENTITY, bias=bias[:, ROPE_HEADS : ROPE_HEADS + 1])
+        nc.scalar.dma_start(out[ROPE_HEADS * HD : HEADS * HD, :], value[:])

@@ -9,6 +9,7 @@ S = 256
 N = 128
 HD = 128
 HALF = HD // 2
+QUARTER = HD // 4
 ROPE_HEADS = 3
 HEADS = ROPE_HEADS + 1
 
@@ -38,13 +39,17 @@ def tile_groupqueryattention_kernel(tc, x, w, b, cosn, sinn, offs, out):
         cos = held.tile([HD, N], F32, name="cos")
         nc.sync.dma_start(cos[:], cosn)
 
-        bias = held.tile([HD, HEADS], F32, name="bias")
-        bias_swapped = held.tile([HD, ROPE_HEADS], F32, name="bias_swapped")
-        b_halves = b.rearrange("(h t p) o -> t p (h o)", t=2, p=HALF)
-        with nc.allow_non_contiguous_dma(reason="one float32 of the bias to a partition"):
-            nc.sync.dma_start(bias[:], b.rearrange("(h p) o -> p (h o)", p=HD))
-            nc.scalar.dma_start(bias_swapped[0:HALF, :], b_halves[1][:, 0:ROPE_HEADS])
-            nc.scalar.dma_start(bias_swapped[HALF:HD, :], b_halves[0][:, 0:ROPE_HEADS])
+        bias_runs = held.tile([HD, 2 * HEADS * QUARTER], F32, name="bias_runs", align_bytes=64)
+        nc.gpsimd.memset(bias_runs[:], 0.0)
+        runs = bias_runs[0:HD:QUARTER, :].rearrange("q (n r) -> q n r", r=QUARTER)
+        b_runs = b.rearrange("(h q r) o -> q h (r o)", q=HD // QUARTER, r=QUARTER)
+        nc.sync.dma_start(runs[:, 0:HEADS, :], b_runs)
+        nc.scalar.dma_start(runs[0:2, HEADS : HEADS + ROPE_HEADS, :], b_runs[2:4, 0:ROPE_HEADS, :])
+        nc.scalar.dma_start(runs[2:4, HEADS : HEADS + ROPE_HEADS, :], b_runs[0:2, 0:ROPE_HEADS, :])
+        bias_blocks = held.tile([HD, 2 * HEADS * QUARTER], F32, name="bias_blocks", align_bytes=64)
+        nc.vector.transpose(bias_blocks[:], bias_runs[:])
+        bias = bias_blocks[:, 0 : HEADS * QUARTER : QUARTER]
+        bias_swapped = bias_blocks[:, HEADS * QUARTER : 2 * HEADS * QUARTER : QUARTER]
 
         scratch = held.tile([HD, 1], F32, name="scratch")
         nc.vector.memset(scratch[:], 0.0)

@@ -39,17 +39,18 @@ def tile_groupqueryattention_kernel(tc, x, w, b, cosn, sinn, offs, out):
         cos = held.tile([HD, N], F32, name="cos")
         nc.sync.dma_start(cos[:], cosn)
 
-        bias_runs = held.tile([HD, 2 * HEADS * QUARTER], F32, name="bias_runs", align_bytes=64)
+        bias_runs = held.tile([HD, HEADS * QUARTER], F32, name="bias_runs", align_bytes=64)
         nc.gpsimd.memset(bias_runs[:], 0.0)
-        runs = bias_runs[0:HD:QUARTER, :].rearrange("q (n r) -> q n r", r=QUARTER)
+        straight_runs = bias_runs[0:HD:QUARTER, :].rearrange("q (h r) -> q h r", r=QUARTER)
+        swapped_runs = bias_runs[1:HD:QUARTER, :].rearrange("q (h r) -> q h r", r=QUARTER)
         b_runs = b.rearrange("(h q r) o -> q h (r o)", q=HD // QUARTER, r=QUARTER)
-        nc.sync.dma_start(runs[:, 0:HEADS, :], b_runs)
-        nc.scalar.dma_start(runs[0:2, HEADS : HEADS + ROPE_HEADS, :], b_runs[2:4, 0:ROPE_HEADS, :])
-        nc.scalar.dma_start(runs[2:4, HEADS : HEADS + ROPE_HEADS, :], b_runs[0:2, 0:ROPE_HEADS, :])
-        bias_blocks = held.tile([HD, 2 * HEADS * QUARTER], F32, name="bias_blocks", align_bytes=64)
+        nc.sync.dma_start(straight_runs, b_runs)
+        nc.scalar.dma_start(swapped_runs[0:2, 0:ROPE_HEADS, :], b_runs[2:4, 0:ROPE_HEADS, :])
+        nc.scalar.dma_start(swapped_runs[2:4, 0:ROPE_HEADS, :], b_runs[0:2, 0:ROPE_HEADS, :])
+        bias_blocks = held.tile([HD, HEADS * QUARTER], F32, name="bias_blocks", align_bytes=64)
         nc.vector.transpose(bias_blocks[:], bias_runs[:])
         bias = bias_blocks[:, 0 : HEADS * QUARTER : QUARTER]
-        bias_swapped = bias_blocks[:, HEADS * QUARTER : 2 * HEADS * QUARTER : QUARTER]
+        bias_swapped = bias_blocks[:, 1 : HEADS * QUARTER : QUARTER]
 
         scratch = held.tile([HD, 1], F32, name="scratch")
         nc.vector.memset(scratch[:], 0.0)

@@ -31,11 +31,11 @@ def tile_groupqueryattention_kernel(tc, x, w, b, cosn, sinn, offs, out):
         weights = held.tile([E, HEADS, HD], BF16, name="weights")
         nc.scalar.dma_start(weights[:], w.rearrange("k (h d) -> k h d", d=HD))
         w_swapped = held.tile([E, ROPE_HEADS, HD], BF16, name="w_swapped")
-        nc.vector.tensor_copy(w_swapped[:, :, 0:HALF], weights[:, 0:ROPE_HEADS, HALF:HD])
+        nc.vector.tensor_scalar_mul(w_swapped[:, :, 0:HALF], weights[:, 0:ROPE_HEADS, HALF:HD], -1.0)
         nc.vector.tensor_copy(w_swapped[:, :, HALF:HD], weights[:, 0:ROPE_HEADS, 0:HALF])
 
-        sin_signed = held.tile([HD, N], F32, name="sin_signed")
-        nc.scalar.dma_start(sin_signed[:], sinn)
+        sin = held.tile([HD, N], F32, name="sin")
+        nc.scalar.dma_start(sin[:], sinn)
         cos = held.tile([HD, N], F32, name="cos")
         nc.sync.dma_start(cos[:], cosn)
 
@@ -51,12 +51,11 @@ def tile_groupqueryattention_kernel(tc, x, w, b, cosn, sinn, offs, out):
         nc.vector.transpose(bias_blocks[:], bias_runs[:])
         bias = bias_blocks[:, 0 : HEADS * QUARTER : QUARTER]
         bias_swapped = bias_blocks[:, 1 : HEADS * QUARTER : QUARTER]
+        nc.vector.tensor_scalar_mul(bias_swapped[0:HALF, :], bias_swapped[0:HALF, :], -1.0)
 
         scratch = held.tile([HD, 1], F32, name="scratch")
         nc.vector.memset(scratch[:], 0.0)
         nc.scalar.activation(scratch[:], scratch[:], IDENTITY)
-
-        nc.vector.tensor_scalar_mul(sin_signed[0:HALF, :], sin_signed[0:HALF, :], -1.0)
 
         picked = tokens[:].indirect(offsets[:])
         by_cos = []
@@ -71,7 +70,7 @@ def tile_groupqueryattention_kernel(tc, x, w, b, cosn, sinn, offs, out):
             nc.tensor.matmul(swapped_ps[:], w_swapped[:, h, :], picked, start=True, stop=True)
             by_sin = work.tile([HD, N], F32, name="by_sin")
             nc.vector.scalar_tensor_tensor(
-                by_sin[:], swapped_ps[:], bias_swapped[:, h : h + 1], sin_signed[:], ADD, MULT
+                by_sin[:], swapped_ps[:], bias_swapped[:, h : h + 1], sin[:], ADD, MULT
             )
             rotated = work.tile([HD, N], F32, name="rotated")
             nc.vector.tensor_tensor(rotated[:], by_cos[h][:], by_sin[:], ADD)

@@ -40,7 +40,7 @@ def tile_groupqueryattention_kernel(tc, x, w, b, cosn, sinn, offs, out):
         nc.sync.dma_start(cos[:], cosn)
 
         bias_runs = held.tile([HD, HEADS * QUARTER], F32, name="bias_runs", align_bytes=64)
-        nc.gpsimd.memset(bias_runs[:], 0.0)
+        nc.vector.memset(bias_runs[:], 0.0)
         straight_runs = bias_runs[0:HD:QUARTER, :].rearrange("q (h r) -> q h r", r=QUARTER)
         swapped_runs = bias_runs[1:HD:QUARTER, :].rearrange("q (h r) -> q h r", r=QUARTER)
         b_runs = b.rearrange("(h q r) o -> q h (r o)", q=HD // QUARTER, r=QUARTER)

@@ -26,10 +26,10 @@ def tile_groupqueryattention_kernel(tc, x, w, b, cosn, sinn, offs, out):
         offsets = held.tile([E, N // 16], U16, name="offsets")
         nc.sync.dma_start(offsets[:], offs)
         tokens = held.tile([E, S], BF16, name="tokens")
-        nc.sync.dma_start(tokens[:], x)
+        nc.scalar.dma_start(tokens[:], x)
 
         weights = held.tile([E, HEADS, HD], BF16, name="weights")
-        nc.scalar.dma_start(weights[:], w.rearrange("k (h d) -> k h d", d=HD))
+        nc.sync.dma_start(weights[:], w.rearrange("k (h d) -> k h d", d=HD))
         w_swapped = held.tile([E, ROPE_HEADS, HD], BF16, name="w_swapped")
         nc.vector.tensor_scalar_mul(w_swapped[:, :, 0:HALF], weights[:, 0:ROPE_HEADS, HALF:HD], -1.0)
         nc.vector.tensor_copy(w_swapped[:, :, HALF:HD], weights[:, 0:ROPE_HEADS, 0:HALF])

@@ -65,6 +65,12 @@ def tile_groupqueryattention_kernel(tc, x, w, b, cosn, sinn, offs, out):
             by_cos.append(work.tile([HD, N], F32, name="by_cos"))
             nc.vector.scalar_tensor_tensor(by_cos[h][:], straight_ps[:], bias[:, h : h + 1], cos[:], ADD, MULT)
 
+        value_ps = psum.tile([HD, N], F32, name="value_ps")
+        nc.tensor.matmul(value_ps[:], weights[:, ROPE_HEADS, :], picked, start=True, stop=True)
+        value = held.tile([HD, N], F32, name="value")
+        nc.scalar.activation(value[:], value_ps[:], IDENTITY, bias=bias[:, ROPE_HEADS : ROPE_HEADS + 1])
+        nc.scalar.dma_start(out[ROPE_HEADS * HD : HEADS * HD, :], value[:])
+
         for h in range(ROPE_HEADS):
             swapped_ps = psum.tile([HD, N], F32, name=f"swapped_ps{h}")
             nc.tensor.matmul(swapped_ps[:], w_swapped[:, h, :], picked, start=True, stop=True)
@@ -74,10 +80,5 @@ def tile_groupqueryattention_kernel(tc, x, w, b, cosn, sinn, offs, out):
             )
             rotated = work.tile([HD, N], F32, name="rotated")
             nc.vector.tensor_tensor(rotated[:], by_cos[h][:], by_sin[:], ADD)
-            nc.sync.dma_start(out[h * HD : (h + 1) * HD, :], rotated[:])
-
-        value_ps = psum.tile([HD, N], F32, name="value_ps")
-        nc.tensor.matmul(value_ps[:], weights[:, ROPE_HEADS, :], picked, start=True, stop=True)
-        value = held.tile([HD, N], F32, name="value")
-        nc.scalar.activation(value[:], value_ps[:], IDENTITY, bias=bias[:, ROPE_HEADS : ROPE_HEADS + 1])
-        nc.scalar.dma_start(out[ROPE_HEADS * HD : HEADS * HD, :], value[:])
+            queue = nc.sync if h % 2 == 0 else nc.scalar
+            queue.dma_start(out[h * HD : (h + 1) * HD, :], rotated[:])

import concourse.mybir as mybir

BF16, F32, U16 = mybir.dt.bfloat16, mybir.dt.float32, mybir.dt.uint16
ADD, MULT = mybir.AluOpType.add, mybir.AluOpType.mult
IDENTITY = mybir.ActivationFunctionType.Identity

E = 128
S = 256
N = 128
HD = 128
HALF = HD // 2
QUARTER = HD // 4
ROPE_HEADS = 3
HEADS = ROPE_HEADS + 1

FLOPS = 2 * E * HEADS * HD * N


def tile_groupqueryattention_kernel(tc, x, w, b, cosn, sinn, offs, out):
    nc = tc.nc
    with (
        tc.tile_pool(name="held", bufs=1) as held,
        tc.tile_pool(name="work", bufs=ROPE_HEADS) as work,
        tc.psum_pool(name="psum", bufs=1) as psum,
    ):
        offsets = held.tile([E, N // 16], U16, name="offsets")
        nc.sync.dma_start(offsets[:], offs)
        tokens = held.tile([E, S], BF16, name="tokens")
        nc.scalar.dma_start(tokens[:], x)

        weights = held.tile([E, HEADS, HD], BF16, name="weights")
        nc.sync.dma_start(weights[:], w.rearrange("k (h d) -> k h d", d=HD))
        w_swapped = held.tile([E, ROPE_HEADS, HD], BF16, name="w_swapped")
        nc.vector.tensor_scalar_mul(w_swapped[:, :, 0:HALF], weights[:, 0:ROPE_HEADS, HALF:HD], -1.0)
        nc.vector.tensor_copy(w_swapped[:, :, HALF:HD], weights[:, 0:ROPE_HEADS, 0:HALF])

        sin = held.tile([HD, N], F32, name="sin")
        nc.scalar.dma_start(sin[:], sinn)
        cos = held.tile([HD, N], F32, name="cos")
        nc.sync.dma_start(cos[:], cosn)

        bias_runs = held.tile([HD, HEADS * QUARTER], F32, name="bias_runs", align_bytes=64)
        nc.vector.memset(bias_runs[:], 0.0)
        straight_runs = bias_runs[0:HD:QUARTER, :].rearrange("q (h r) -> q h r", r=QUARTER)
        swapped_runs = bias_runs[1:HD:QUARTER, :].rearrange("q (h r) -> q h r", r=QUARTER)
        b_runs = b.rearrange("(h q r) o -> q h (r o)", q=HD // QUARTER, r=QUARTER)
        nc.sync.dma_start(straight_runs, b_runs)
        nc.scalar.dma_start(swapped_runs[0:2, 0:ROPE_HEADS, :], b_runs[2:4, 0:ROPE_HEADS, :])
        nc.scalar.dma_start(swapped_runs[2:4, 0:ROPE_HEADS, :], b_runs[0:2, 0:ROPE_HEADS, :])
        bias_blocks = held.tile([HD, HEADS * QUARTER], F32, name="bias_blocks", align_bytes=64)
        nc.vector.transpose(bias_blocks[:], bias_runs[:])
        bias = bias_blocks[:, 0 : HEADS * QUARTER : QUARTER]
        bias_swapped = bias_blocks[:, 1 : HEADS * QUARTER : QUARTER]
        nc.vector.tensor_scalar_mul(bias_swapped[0:HALF, :], bias_swapped[0:HALF, :], -1.0)

        scratch = held.tile([HD, 1], F32, name="scratch")
        nc.vector.memset(scratch[:], 0.0)
        nc.scalar.activation(scratch[:], scratch[:], IDENTITY)

        picked = tokens[:].indirect(offsets[:])
        by_cos = []
        for h in range(ROPE_HEADS):
            straight_ps = psum.tile([HD, N], F32, name=f"straight_ps{h}")
            nc.tensor.matmul(straight_ps[:], weights[:, h, :], picked, start=True, stop=True)
            by_cos.append(work.tile([HD, N], F32, name="by_cos"))
            nc.vector.scalar_tensor_tensor(by_cos[h][:], straight_ps[:], bias[:, h : h + 1], cos[:], ADD, MULT)

        value_ps = psum.tile([HD, N], F32, name="value_ps")
        nc.tensor.matmul(value_ps[:], weights[:, ROPE_HEADS, :], picked, start=True, stop=True)
        value = held.tile([HD, N], F32, name="value")
        nc.scalar.activation(value[:], value_ps[:], IDENTITY, bias=bias[:, ROPE_HEADS : ROPE_HEADS + 1])
        nc.scalar.dma_start(out[ROPE_HEADS * HD : HEADS * HD, :], value[:])

        for h in range(ROPE_HEADS):
            swapped_ps = psum.tile([HD, N], F32, name=f"swapped_ps{h}")
            nc.tensor.matmul(swapped_ps[:], w_swapped[:, h, :], picked, start=True, stop=True)
            by_sin = work.tile([HD, N], F32, name="by_sin")
            nc.vector.scalar_tensor_tensor(
                by_sin[:], swapped_ps[:], bias_swapped[:, h : h + 1], sin[:], ADD, MULT
            )
            rotated = work.tile([HD, N], F32, name="rotated")
            nc.vector.tensor_tensor(rotated[:], by_cos[h][:], by_sin[:], ADD)
            queue = nc.sync if h % 2 == 0 else nc.scalar
            queue.dma_start(out[h * HD : (h + 1) * HD, :], rotated[:])
